import numpy as np
import ml_dtypes


def mxq(x, axis, fmt="e4m3"):
    dtype, down = {"e4m3": (ml_dtypes.float8_e4m3fn, 7), "e5m2": (ml_dtypes.float8_e5m2, 14)}[fmt]
    v = np.moveaxis(np.asarray(x, np.float32).astype(ml_dtypes.bfloat16).astype(np.float64), axis, -1)
    blocks = v.reshape(v.shape[:-1] + (-1, 32))
    amax = np.abs(blocks).max(-1, keepdims=True)
    byte = np.maximum(np.where(amax > 0, np.frexp(amax)[1] - 1 + 127, 0) - down, 1)
    scale = np.exp2(byte - 127.0)
    codes = (blocks / scale).astype(np.float32).astype(dtype).astype(np.float64)
    return np.moveaxis((codes * scale).reshape(v.shape), -1, axis)


WIDE = False


def mx_kscale(k):
    if not WIDE:
        return np.ones(k)
    levels = np.array([20, -20, 10, -10, 0])
    a = np.random.permutation(np.resize(levels, k // 512 * 4)).reshape(k // 512, 4)
    idx = np.arange(k)
    return np.exp2(a[idx // 512, idx % 128 // 32])


BF16 = ml_dtypes.bfloat16


def bf(x):
    return np.asarray(x, np.float32).astype(BF16)


def f64(x):
    return np.asarray(x).astype(np.float64)


B, G, DB, DR = 512, 8, 1024, 2048


def mish(v):
    return v * np.tanh(np.log(1.0 + np.exp(v)))


def dmish(v):
    th = np.tanh(np.log(1.0 + np.exp(v)))
    return th + v * (1.0 - th * th) / (1.0 + np.exp(-v))


def setup_inputs():
    u = mx_kscale(DR)
    BB_feature = bf(np.random.standard_normal((B, G, DB)))
    RF_feature = bf(np.random.standard_normal((B, DR)))
    W0 = bf(np.random.standard_normal((DR, DR)) / np.sqrt(DR))
    b_rfrf = bf(np.random.standard_normal(DR) * 0.5)
    W_bbrf = bf(np.random.standard_normal((DR, DB)) * np.sqrt(G / DB))
    b_bbrf = bf(np.random.standard_normal(DR) * 0.5)
    g = bf(np.random.standard_normal((B, DR)) * np.exp2(np.random.randint(-12, 1, (B, 1))) * 32.0 * u)
    z_rf = f64(RF_feature) @ f64(W0).T + f64(b_rfrf)
    return {"BB_feature": BB_feature,
            "RF_feature": RF_feature,
            "W_rfrf": bf(f64(W0) / u[:, None]),
            "b_rfrf": b_rfrf,
            "W_bbrf": W_bbrf,
            "b_bbrf": b_bbrf,
            "z_rf": np.asarray(z_rf, np.float32),
            "grad_out": g}


def reference(BB_feature, RF_feature, W_rfrf, b_rfrf, W_bbrf, b_bbrf, z_rf, grad_out):
    dz = f64(grad_out) * dmish(f64(z_rf))
    return mxq(dz, 1, "e5m2") @ mxq(f64(W_rfrf), 0, "e4m3")

@@ -1,0 +1,224 @@
+from contextlib import ExitStack
+
+import concourse.mybir as mybir
+from concourse.masks import make_identity
+
+F32 = mybir.dt.float32
+BF16 = mybir.dt.bfloat16
+U32 = mybir.dt.uint32
+U8 = mybir.dt.uint8
+E4M3_X4 = mybir.dt.float8_e4m3fn_x4
+E5M2_X4 = mybir.dt.float8_e5m2_x4
+ACT = mybir.ActivationFunctionType
+ALU = mybir.AluOpType
+
+P = 128
+PACK = 4
+K_PASS = P * PACK
+BATCH = 512
+DR = 2048
+B_TILES = BATCH // P
+PASSES = DR // K_PASS
+N_TILE = 512
+N_TILES = DR // N_TILE
+W_COLS = 1024
+W_CHUNKS = PASSES * (DR // W_COLS)
+PAIR = 2
+UNITS = B_TILES * (PASSES // PAIR)
+AHEAD = 2
+TANH_CAP = 1.0 - 2.0**-24
+
+FLOPS = 2 * BATCH * DR * DR
+BYTES = 2 * DR * DR + (4 + 2 + 4) * BATCH * DR
+
+
+def tile_gnn_layer_pa_v_kernel(
+    tc, BB_feature, RF_feature, W_rfrf, b_rfrf, W_bbrf, b_bbrf, z_rf, grad_out, out
+):
+    nc = tc.nc
+    with ExitStack() as stack:
+        keep = stack.enter_context(tc.tile_pool(name="keep", bufs=1))
+        z_pool = stack.enter_context(tc.tile_pool(name="z_pool", bufs=8))
+        w_pool = stack.enter_context(tc.tile_pool(name="w_pool", bufs=3))
+        wg_pool = stack.enter_context(tc.tile_pool(name="wg_pool", bufs=2))
+        u_pool = stack.enter_context(tc.tile_pool(name="u_pool", bufs=AHEAD + 2))
+        dz_pool = stack.enter_context(tc.tile_pool(name="dz_pool", bufs=2))
+        o_pool = stack.enter_context(tc.tile_pool(name="o_pool", bufs=4))
+        psum_z = stack.enter_context(tc.psum_pool(name="psum_z", bufs=2))
+        psum_g = stack.enter_context(tc.psum_pool(name="psum_g", bufs=2))
+        psum_o = stack.enter_context(tc.psum_pool(name="psum_o", bufs=N_TILES))
+        stack.enter_context(tc.manual_schedule())
+
+        ident_f32 = keep.tile([P, P], F32, name="ident_f32")
+        make_identity(nc, ident_f32[:])
+        ident_bf16 = keep.tile([P, P], BF16, name="ident_bf16")
+        make_identity(nc, ident_bf16[:])
+        half = keep.tile([P, 1], F32, name="half")
+        nc.vector.memset(half[:], 0.5)
+
+        def rows(bt):
+            return slice(bt * P, (bt + 1) * P)
+
+        def load_w(i):
+            c, h = divmod(i, DR // W_COLS)
+            raw = w_pool.tile([P, PACK, W_COLS], BF16, name="w_raw")
+            nc.sync.dma_start(
+                out=raw[:],
+                in_=W_rfrf[c * K_PASS : (c + 1) * K_PASS, h * W_COLS : (h + 1) * W_COLS].rearrange(
+                    "(t p) n -> p t n", p=P
+                ),
+            )
+            return raw
+
+        z_piece = {}
+        w_raw = {}
+        for bt in range(B_TILES):
+            for c in range(PASSES):
+                z_piece[bt, c] = z_pool.tile([P, K_PASS], F32, name="z_piece")
+                nc.sync.dma_start(
+                    out=z_piece[bt, c][:], in_=z_rf[rows(bt), c * K_PASS : (c + 1) * K_PASS]
+                )
+                if c == 0:
+                    w_raw[bt] = load_w(bt)
+        for i in range(B_TILES, W_CHUNKS):
+            w_raw[i] = load_w(i)
+        grad = []
+        for bt in range(B_TILES):
+            grad.append(keep.tile([P, DR], BF16, name="grad%d" % bt))
+            nc.sync.dma_start(out=grad[bt][:], in_=grad_out[rows(bt), :])
+
+        silu = [keep.tile([P, PASSES, PACK, P], F32, name="silu%d" % bt) for bt in range(B_TILES)]
+        chain = [keep.tile([P, PASSES, PACK, P], F32, name="chain%d" % bt) for bt in range(B_TILES)]
+        for bt in range(B_TILES):
+            for c in range(PASSES):
+                z_t = psum_z.tile([P, PACK, P], F32, name="z_t")
+                for t in range(PACK):
+                    nc.tensor.transpose(
+                        z_t[:, t, :], z_piece[bt, c][:, t * P : (t + 1) * P], ident_f32[:]
+                    )
+                nc.scalar.activation(out=silu[bt][:, c], in_=z_t[:], func=ACT.Silu)
+                nc.scalar.activation(out=chain[bt][:, c], in_=z_t[:], func=ACT.Tanh, scale=0.5)
+
+        w_codes = [keep.tile([P, DR], U32, name="w_codes%d" % c, align_bytes=64) for c in range(PASSES)]
+        w_scales = [keep.tile([P, DR], U8, name="w_scales%d" % c, align_bytes=64) for c in range(PASSES)]
+        w_grouped = {}
+
+        def regroup_w(i):
+            w_grouped[i] = wg_pool.tile([P, W_COLS, PACK], BF16, name="w_grouped", align_bytes=64)
+            nc.vector.tensor_copy(
+                out=w_grouped[i][:].rearrange("p (q i) t -> p q t i", i=4),
+                in_=w_raw[i][:].rearrange("p t (q i) -> p q t i", i=4),
+            )
+
+        def quantise_w(i):
+            c, h = divmod(i, DR // W_COLS)
+            cols = slice(h * W_COLS, (h + 1) * W_COLS)
+            nc.vector.quantize_mx(
+                out=w_codes[c][:, cols].bitcast(E4M3_X4),
+                scales=w_scales[c][:, cols],
+                in_=w_grouped[i][:].rearrange("p n t -> p (n t)"),
+            )
+
+        for i in range(W_CHUNKS):
+            regroup_w(i)
+            if i > 0:
+                quantise_w(i - 1)
+            if i < B_TILES:
+                nc.vector.tensor_scalar_min(out=chain[i][:], in0=chain[i][:], scalar1=TANH_CAP)
+        quantise_w(W_CHUNKS - 1)
+
+        for bt in range(B_TILES):
+            nc.scalar.activation(
+                out=chain[bt][:], in_=chain[bt][:], func=ACT.Ln, scale=-0.5, bias=half[:]
+            )
+
+        dz_codes = [keep.tile([P, PASSES * P], U32, name="dz_codes%d" % bt, align_bytes=64) for bt in range(B_TILES)]
+        dz_scales = [keep.tile([P, PASSES * P], U8, name="dz_scales%d" % bt, align_bytes=64) for bt in range(B_TILES)]
+        work = {}
+        grad_t = {}
+        dz_grouped = {}
+        acc = {}
+
+        def part(tiles, s):
+            bt, hc = divmod(s, PASSES // PAIR)
+            return tiles[bt][:, hc * PAIR : (hc + 1) * PAIR]
+
+        def tanh_and_square(s):
+            nc.scalar.activation(out=part(chain, s), in_=part(chain, s), func=ACT.Tanh, scale=-1.0)
+            work[s] = u_pool.tile([P, PAIR, PACK, P], F32, name="work")
+            nc.scalar.activation(out=work[s][:], in_=part(chain, s), func=ACT.Square)
+
+        def transpose_grad(s):
+            bt, hc = divmod(s, PASSES // PAIR)
+            grad_t[s] = psum_g.tile([P, PAIR, PACK, P], BF16, name="grad_t")
+            for cc in range(PAIR):
+                for t in range(PACK):
+                    k0 = (hc * PAIR + cc) * K_PASS + t * P
+                    nc.tensor.transpose(grad_t[s][:, cc, t, :], grad[bt][:, k0 : k0 + P], ident_bf16[:])
+
+        def slope_term(s):
+            nc.vector.scalar_tensor_tensor(
+                out=work[s][:], in0=work[s][:], scalar=1.0, in1=part(silu, s),
+                op0=ALU.subtract, op1=ALU.mult,
+            )
+
+        def derivative(s):
+            nc.vector.tensor_tensor(out=work[s][:], in0=part(chain, s), in1=work[s][:], op=ALU.subtract)
+
+        def times_grad(s):
+            dz_grouped[s] = dz_pool.tile([P, PAIR, P, PACK], BF16, name="dz_grouped", align_bytes=64)
+            nc.vector.tensor_tensor(
+                out=dz_grouped[s][:],
+                in0=work[s][:].rearrange("p c t b -> p c b t"),
+                in1=grad_t[s][:].rearrange("p c t b -> p c b t"),
+                op=ALU.mult,
+            )
+
+        def quantise_dz(s):
+            bt, hc = divmod(s, PASSES // PAIR)
+            cols = slice(hc * PAIR * P, (hc + 1) * PAIR * P)
+            nc.vector.quantize_mx(
+                out=dz_codes[bt][:, cols].bitcast(E5M2_X4),
+                scales=dz_scales[bt][:, cols],
+                in_=dz_grouped[s][:].rearrange("p c b t -> p (c b t)"),
+            )
+
+        def multiply(s):
+            bt, hc = divmod(s, PASSES // PAIR)
+            for j in range(N_TILES):
+                if hc == 0:
+                    acc[bt, j] = psum_o.tile([P, N_TILE], F32, name="acc")
+                for c in range(hc * PAIR, (hc + 1) * PAIR):
+                    nc.tensor.matmul_mx(
+                        out=acc[bt, j][:],
+                        lhsT=dz_codes[bt][:, c * P : (c + 1) * P].bitcast(E5M2_X4),
+                        lhsT_scale=dz_scales[bt][:, c * P : (c + 1) * P],
+                        rhs=w_codes[c][:, j * N_TILE : (j + 1) * N_TILE].bitcast(E4M3_X4),
+                        rhs_scale=w_scales[c][:, j * N_TILE : (j + 1) * N_TILE],
+                        start=(c == 0),
+                        stop=(c == PASSES - 1),
+                    )
+
+        def store_rows(bt):
+            for j in range(N_TILES):
+                o_sb = o_pool.tile([P, N_TILE], F32, name="o_sb")
+                nc.scalar.copy(out=o_sb[:], in_=acc[bt, j][:])
+                nc.sync.dma_start(out=out[rows(bt), j * N_TILE : (j + 1) * N_TILE], in_=o_sb[:])
+
+        for step in range(UNITS + AHEAD + 1):
+            front = step - AHEAD
+            back = front - 1
+            if step < UNITS:
+                tanh_and_square(step)
+            if 0 <= front < UNITS:
+                transpose_grad(front)
+                slope_term(front)
+            if 0 <= back:
+                times_grad(back)
+            if 0 <= front < UNITS:
+                derivative(front)
+            if 0 <= back:
+                quantise_dz(back)
+                multiply(back)
+                if back % (PASSES // PAIR) == PASSES // PAIR - 1:
+                    store_rows(back // (PASSES // PAIR))

@@ -87,8 +87,8 @@ def tile_gnn_layer_pa_v_kernel(
             grad.append(keep.tile([P, DR], BF16, name="grad%d" % bt))
             nc.sync.dma_start(out=grad[bt][:], in_=grad_out[rows(bt), :])
 
-        silu = [keep.tile([P, PASSES, PACK, P], F32, name="silu%d" % bt) for bt in range(B_TILES)]
-        chain = [keep.tile([P, PASSES, PACK, P], F32, name="chain%d" % bt) for bt in range(B_TILES)]
+        silu = [keep.tile([P, PASSES, P, PACK], F32, name="silu%d" % bt) for bt in range(B_TILES)]
+        chain = [keep.tile([P, PASSES, P, PACK], F32, name="chain%d" % bt) for bt in range(B_TILES)]
         for bt in range(B_TILES):
             for c in range(PASSES):
                 z_t = psum_z.tile([P, PACK, P], F32, name="z_t")
@@ -96,8 +96,9 @@ def tile_gnn_layer_pa_v_kernel(
                     nc.tensor.transpose(
                         z_t[:, t, :], z_piece[bt, c][:, t * P : (t + 1) * P], ident_f32[:]
                     )
-                nc.scalar.activation(out=silu[bt][:, c], in_=z_t[:], func=ACT.Silu)
-                nc.scalar.activation(out=chain[bt][:, c], in_=z_t[:], func=ACT.Tanh, scale=0.5)
+                z_words = z_t[:].rearrange("p t b -> p b t")
+                nc.scalar.activation(out=silu[bt][:, c], in_=z_words, func=ACT.Silu)
+                nc.scalar.activation(out=chain[bt][:, c], in_=z_words, func=ACT.Tanh, scale=0.5)
 
         w_codes = [keep.tile([P, DR], U32, name="w_codes%d" % c, align_bytes=64) for c in range(PASSES)]
         w_scales = [keep.tile([P, DR], U8, name="w_scales%d" % c, align_bytes=64) for c in range(PASSES)]
@@ -143,9 +144,11 @@ def tile_gnn_layer_pa_v_kernel(
             bt, hc = divmod(s, PASSES // PAIR)
             return tiles[bt][:, hc * PAIR : (hc + 1) * PAIR]
 
-        def tanh_and_square(s):
+        def tanh_softplus(s):
             nc.scalar.activation(out=part(chain, s), in_=part(chain, s), func=ACT.Tanh, scale=-1.0)
-            work[s] = u_pool.tile([P, PAIR, PACK, P], F32, name="work")
+
+        def square(s):
+            work[s] = u_pool.tile([P, PAIR, P, PACK], F32, name="work")
             nc.scalar.activation(out=work[s][:], in_=part(chain, s), func=ACT.Square)
 
         def transpose_grad(s):
@@ -169,7 +172,7 @@ def tile_gnn_layer_pa_v_kernel(
             dz_grouped[s] = dz_pool.tile([P, PAIR, P, PACK], BF16, name="dz_grouped", align_bytes=64)
             nc.vector.tensor_tensor(
                 out=dz_grouped[s][:],
-                in0=work[s][:].rearrange("p c t b -> p c b t"),
+                in0=work[s][:],
                 in1=grad_t[s][:].rearrange("p c t b -> p c b t"),
                 op=ALU.mult,
             )
@@ -205,11 +208,13 @@ def tile_gnn_layer_pa_v_kernel(
                 nc.scalar.copy(out=o_sb[:], in_=acc[bt, j][:])
                 nc.sync.dma_start(out=out[rows(bt), j * N_TILE : (j + 1) * N_TILE], in_=o_sb[:])
 
-        for step in range(UNITS + AHEAD + 1):
-            front = step - AHEAD
+        for step in range(UNITS + AHEAD + 2):
+            front = step - 1 - AHEAD
             back = front - 1
             if step < UNITS:
-                tanh_and_square(step)
+                tanh_softplus(step)
+            if 0 <= step - 1 < UNITS:
+                square(step - 1)
             if 0 <= front < UNITS:
                 transpose_grad(front)
                 slope_term(front)

@@ -44,8 +44,7 @@ def tile_gnn_layer_pa_v_kernel(
         u_pool = stack.enter_context(tc.tile_pool(name="u_pool", bufs=AHEAD + 2))
         dz_pool = stack.enter_context(tc.tile_pool(name="dz_pool", bufs=2))
         o_pool = stack.enter_context(tc.tile_pool(name="o_pool", bufs=4))
-        psum_z = stack.enter_context(tc.psum_pool(name="psum_z", bufs=2))
-        psum_g = stack.enter_context(tc.psum_pool(name="psum_g", bufs=2))
+        psum_t = stack.enter_context(tc.psum_pool(name="psum_t", bufs=4))
         psum_o = stack.enter_context(tc.psum_pool(name="psum_o", bufs=N_TILES))
         stack.enter_context(tc.manual_schedule())
 
@@ -91,7 +90,7 @@ def tile_gnn_layer_pa_v_kernel(
         chain = [keep.tile([P, PASSES, P, PACK], F32, name="chain%d" % bt) for bt in range(B_TILES)]
         for bt in range(B_TILES):
             for c in range(PASSES):
-                z_t = psum_z.tile([P, PACK, P], F32, name="z_t")
+                z_t = psum_t.tile([P, PACK, P], F32, name="z_t", tag="transposed")
                 for t in range(PACK):
                     nc.tensor.transpose(
                         z_t[:, t, :], z_piece[bt, c][:, t * P : (t + 1) * P], ident_f32[:]
@@ -153,7 +152,7 @@ def tile_gnn_layer_pa_v_kernel(
 
         def transpose_grad(s):
             bt, hc = divmod(s, PASSES // PAIR)
-            grad_t[s] = psum_g.tile([P, PAIR, PACK, P], BF16, name="grad_t")
+            grad_t[s] = psum_t.tile([P, PAIR, PACK, P], BF16, name="grad_t", tag="transposed")
             for cc in range(PAIR):
                 for t in range(PACK):
                     k0 = (hc * PAIR + cc) * K_PASS + t * P
@@ -215,8 +214,9 @@ def tile_gnn_layer_pa_v_kernel(
                 tanh_softplus(step)
             if 0 <= step - 1 < UNITS:
                 square(step - 1)
+            if 0 <= front + 1 < UNITS:
+                transpose_grad(front + 1)
             if 0 <= front < UNITS:
-                transpose_grad(front)
                 slope_term(front)
             if 0 <= back:
                 times_grad(back)

@@ -52,6 +52,8 @@ def tile_gnn_layer_pa_v_kernel(
         make_identity(nc, ident_f32[:])
         ident_bf16 = keep.tile([P, P], BF16, name="ident_bf16")
         make_identity(nc, ident_bf16[:])
+        minus_four = keep.tile([P, P], BF16, name="minus_four")
+        nc.vector.tensor_scalar_mul(out=minus_four[:], in0=ident_bf16[:], scalar1=-4.0)
         half = keep.tile([P, 1], F32, name="half")
         nc.vector.memset(half[:], 0.5)
 
@@ -143,37 +145,48 @@ def tile_gnn_layer_pa_v_kernel(
             bt, hc = divmod(s, PASSES // PAIR)
             return tiles[bt][:, hc * PAIR : (hc + 1) * PAIR]
 
-        def tanh_softplus(s):
-            nc.scalar.activation(out=part(chain, s), in_=part(chain, s), func=ACT.Tanh, scale=-1.0)
-
-        def square(s):
-            work[s] = u_pool.tile([P, PAIR, P, PACK], F32, name="work")
-            nc.scalar.activation(out=work[s][:], in_=part(chain, s), func=ACT.Square)
+        def ratio(s):
+            nc.scalar.activation(out=part(chain, s), in_=part(chain, s), func=ACT.Sigmoid, scale=-2.0)
 
         def transpose_grad(s):
             bt, hc = divmod(s, PASSES // PAIR)
-            grad_t[s] = psum_t.tile([P, PAIR, PACK, P], BF16, name="grad_t", tag="transposed")
+            grad_t[s] = psum_t.tile([P, PACK, PAIR * P], BF16, name="grad_t", tag="transposed")
             for cc in range(PAIR):
                 for t in range(PACK):
                     k0 = (hc * PAIR + cc) * K_PASS + t * P
-                    nc.tensor.transpose(grad_t[s][:, cc, t, :], grad[bt][:, k0 : k0 + P], ident_bf16[:])
+                    nc.tensor.matmul(
+                        grad_t[s][:, t, cc * P : (cc + 1) * P], lhsT=grad[bt][:, k0 : k0 + P], rhs=minus_four[:],
+                        start=True, stop=True,
+                    )
 
         def slope_term(s):
+            work[s] = u_pool.tile([P, PAIR, P, PACK], F32, name="work")
             nc.vector.scalar_tensor_tensor(
-                out=work[s][:], in0=work[s][:], scalar=1.0, in1=part(silu, s),
+                out=work[s][:].rearrange("p c b t -> p (c b t)"),
+                in0=part(chain, s).rearrange("p c b t -> p (c b t)"),
+                scalar=1.0,
+                in1=part(silu, s).rearrange("p c b t -> p (c b t)"),
                 op0=ALU.subtract, op1=ALU.mult,
             )
 
         def derivative(s):
-            nc.vector.tensor_tensor(out=work[s][:], in0=part(chain, s), in1=work[s][:], op=ALU.subtract)
+            nc.vector.scalar_tensor_tensor(
+                out=work[s][:].rearrange("p c b t -> p (c b t)"),
+                in0=work[s][:].rearrange("p c b t -> p (c b t)"),
+                scalar=0.5,
+                in1=part(chain, s).rearrange("p c b t -> p (c b t)"),
+                op0=ALU.subtract, op1=ALU.mult,
+            )
 
         def times_grad(s):
-            dz_grouped[s] = dz_pool.tile([P, PAIR, P, PACK], BF16, name="dz_grouped", align_bytes=64)
-            nc.vector.tensor_tensor(
+            dz_grouped[s] = dz_pool.tile([P, PAIR * P, PACK], BF16, name="dz_grouped", align_bytes=64)
+            nc.vector.scalar_tensor_tensor(
                 out=dz_grouped[s][:],
-                in0=work[s][:],
-                in1=grad_t[s][:].rearrange("p c t b -> p c b t"),
-                op=ALU.mult,
+                in0=work[s][:].rearrange("p c b t -> p (c b) t"),
+                scalar=0.25,
+                in1=grad_t[s][:].rearrange("p t x -> p x t"),
+                op0=ALU.add,
+                op1=ALU.mult,
             )
 
         def quantise_dz(s):
@@ -182,7 +195,7 @@ def tile_gnn_layer_pa_v_kernel(
             nc.vector.quantize_mx(
                 out=dz_codes[bt][:, cols].bitcast(E5M2_X4),
                 scales=dz_scales[bt][:, cols],
-                in_=dz_grouped[s][:].rearrange("p c b t -> p (c b t)"),
+                in_=dz_grouped[s][:].rearrange("p x t -> p (x t)"),
             )
 
         def multiply(s):
@@ -207,13 +220,11 @@ def tile_gnn_layer_pa_v_kernel(
                 nc.scalar.copy(out=o_sb[:], in_=acc[bt, j][:])
                 nc.sync.dma_start(out=out[rows(bt), j * N_TILE : (j + 1) * N_TILE], in_=o_sb[:])
 
-        for step in range(UNITS + AHEAD + 2):
-            front = step - 1 - AHEAD
+        for step in range(UNITS + AHEAD + 1):
+            front = step - AHEAD
             back = front - 1
             if step < UNITS:
-                tanh_softplus(step)
-            if 0 <= step - 1 < UNITS:
-                square(step - 1)
+                ratio(step)
             if 0 <= front + 1 < UNITS:
                 transpose_grad(front + 1)
             if 0 <= front < UNITS:

@@ -21,11 +21,7 @@ B_TILES = BATCH // P
 PASSES = DR // K_PASS
 N_TILE = 512
 N_TILES = DR // N_TILE
-W_COLS = 1024
-W_CHUNKS = PASSES * (DR // W_COLS)
-PAIR = 2
-UNITS = B_TILES * (PASSES // PAIR)
-AHEAD = 2
+HALF_W = 1024
 TANH_CAP = 1.0 - 2.0**-24
 
 FLOPS = 2 * BATCH * DR * DR
@@ -41,200 +37,240 @@ def tile_gnn_layer_pa_v_kernel(
         z_pool = stack.enter_context(tc.tile_pool(name="z_pool", bufs=8))
         w_pool = stack.enter_context(tc.tile_pool(name="w_pool", bufs=3))
         wg_pool = stack.enter_context(tc.tile_pool(name="wg_pool", bufs=2))
-        u_pool = stack.enter_context(tc.tile_pool(name="u_pool", bufs=AHEAD + 2))
+        u_pool = stack.enter_context(tc.tile_pool(name="u_pool", bufs=3))
         dz_pool = stack.enter_context(tc.tile_pool(name="dz_pool", bufs=2))
         o_pool = stack.enter_context(tc.tile_pool(name="o_pool", bufs=4))
-        psum_t = stack.enter_context(tc.psum_pool(name="psum_t", bufs=4))
-        psum_o = stack.enter_context(tc.psum_pool(name="psum_o", bufs=N_TILES))
+        psum_t = stack.enter_context(tc.psum_pool(name="psum_t", bufs=2))
+        psum_o = stack.enter_context(tc.psum_pool(name="psum_o", bufs=6))
         stack.enter_context(tc.manual_schedule())
 
         ident_f32 = keep.tile([P, P], F32, name="ident_f32")
         make_identity(nc, ident_f32[:])
-        ident_bf16 = keep.tile([P, P], BF16, name="ident_bf16")
-        make_identity(nc, ident_bf16[:])
         minus_four = keep.tile([P, P], BF16, name="minus_four")
-        nc.vector.tensor_scalar_mul(out=minus_four[:], in0=ident_bf16[:], scalar1=-4.0)
+        nc.vector.tensor_scalar_mul(out=minus_four[:], in0=ident_f32[:], scalar1=-4.0)
         half = keep.tile([P, 1], F32, name="half")
         nc.vector.memset(half[:], 0.5)
 
         def rows(bt):
             return slice(bt * P, (bt + 1) * P)
 
-        def load_w(i):
-            c, h = divmod(i, DR // W_COLS)
-            raw = w_pool.tile([P, PACK, W_COLS], BF16, name="w_raw")
+        w_pieces = [(0, 0, 512), (0, 512, 512), (0, HALF_W, HALF_W)]
+        w_pieces += [(c, h * HALF_W, HALF_W) for c in range(1, PASSES) for h in range(2)]
+        w_raw = []
+        z_piece = []
+
+        def load_w():
+            c, n0, width = w_pieces[len(w_raw)]
+            raw = w_pool.tile([P, PACK, width], BF16, name="w_raw")
             nc.sync.dma_start(
                 out=raw[:],
-                in_=W_rfrf[c * K_PASS : (c + 1) * K_PASS, h * W_COLS : (h + 1) * W_COLS].rearrange(
+                in_=W_rfrf[c * K_PASS : (c + 1) * K_PASS, n0 : n0 + width].rearrange(
                     "(t p) n -> p t n", p=P
                 ),
             )
-            return raw
+            w_raw.append(raw)
 
-        z_piece = {}
-        w_raw = {}
-        for bt in range(B_TILES):
-            for c in range(PASSES):
-                z_piece[bt, c] = z_pool.tile([P, K_PASS], F32, name="z_piece")
-                nc.sync.dma_start(
-                    out=z_piece[bt, c][:], in_=z_rf[rows(bt), c * K_PASS : (c + 1) * K_PASS]
-                )
-                if c == 0:
-                    w_raw[bt] = load_w(bt)
-        for i in range(B_TILES, W_CHUNKS):
-            w_raw[i] = load_w(i)
+        def load_z():
+            bt, c = divmod(len(z_piece), PASSES)
+            piece = z_pool.tile([P, K_PASS], F32, name="z_piece")
+            nc.sync.dma_start(out=piece[:], in_=z_rf[rows(bt), c * K_PASS : (c + 1) * K_PASS])
+            z_piece.append(piece)
+
+        for kind in "zwzwzzwzzzwzzzwzzzwzzzwww":
+            if kind == "z":
+                load_z()
+            else:
+                load_w()
         grad = []
         for bt in range(B_TILES):
             grad.append(keep.tile([P, DR], BF16, name="grad%d" % bt))
             nc.sync.dma_start(out=grad[bt][:], in_=grad_out[rows(bt), :])
 
-        silu = [keep.tile([P, PASSES, P, PACK], F32, name="silu%d" % bt) for bt in range(B_TILES)]
-        chain = [keep.tile([P, PASSES, P, PACK], F32, name="chain%d" % bt) for bt in range(B_TILES)]
-        for bt in range(B_TILES):
-            for c in range(PASSES):
-                z_t = psum_t.tile([P, PACK, P], F32, name="z_t", tag="transposed")
-                for t in range(PACK):
-                    nc.tensor.transpose(
-                        z_t[:, t, :], z_piece[bt, c][:, t * P : (t + 1) * P], ident_f32[:]
-                    )
-                z_words = z_t[:].rearrange("p t b -> p b t")
-                nc.scalar.activation(out=silu[bt][:, c], in_=z_words, func=ACT.Silu)
-                nc.scalar.activation(out=chain[bt][:, c], in_=z_words, func=ACT.Tanh, scale=0.5)
+        silu = [keep.tile([P, PASSES * P * PACK], F32, name="silu%d" % bt) for bt in range(B_TILES)]
+        chain = [keep.tile([P, PASSES * P * PACK], F32, name="chain%d" % bt) for bt in range(B_TILES)]
+
+        def z_functions(i):
+            bt, c = divmod(i, PASSES)
+            cols = slice(c * K_PASS, (c + 1) * K_PASS)
+            z_t = psum_t.tile([P, PACK, P], F32, name="z_t", tag="transposed")
+            for t in range(PACK):
+                nc.tensor.transpose(z_t[:, t, :], z_piece[i][:, t * P : (t + 1) * P], ident_f32[:])
+            z_words = z_t[:].rearrange("p t b -> p b t")
+            for dest, func, scale in ((silu, ACT.Silu, 1.0), (chain, ACT.Tanh, 0.5)):
+                nc.scalar.activation(
+                    out=dest[bt][:, cols].rearrange("p (b t) -> p b t", t=PACK),
+                    in_=z_words, func=func, scale=scale,
+                )
 
         w_codes = [keep.tile([P, DR], U32, name="w_codes%d" % c, align_bytes=64) for c in range(PASSES)]
         w_scales = [keep.tile([P, DR], U8, name="w_scales%d" % c, align_bytes=64) for c in range(PASSES)]
         w_grouped = {}
 
-        def regroup_w(i):
-            w_grouped[i] = wg_pool.tile([P, W_COLS, PACK], BF16, name="w_grouped", align_bytes=64)
-            nc.vector.tensor_copy(
+        def regroup_w(i, copy):
+            width = w_pieces[i][2]
+            w_grouped[i] = wg_pool.tile([P, width, PACK], BF16, name="w_grouped", align_bytes=64)
+            copy(
                 out=w_grouped[i][:].rearrange("p (q i) t -> p q t i", i=4),
                 in_=w_raw[i][:].rearrange("p t (q i) -> p q t i", i=4),
             )
 
         def quantise_w(i):
-            c, h = divmod(i, DR // W_COLS)
-            cols = slice(h * W_COLS, (h + 1) * W_COLS)
+            c, n0, width = w_pieces[i]
             nc.vector.quantize_mx(
-                out=w_codes[c][:, cols].bitcast(E4M3_X4),
-                scales=w_scales[c][:, cols],
+                out=w_codes[c][:, n0 : n0 + width].bitcast(E4M3_X4),
+                scales=w_scales[c][:, n0 : n0 + width],
                 in_=w_grouped[i][:].rearrange("p n t -> p (n t)"),
             )
 
-        for i in range(W_CHUNKS):
-            regroup_w(i)
-            if i > 0:
-                quantise_w(i - 1)
-            if i < B_TILES:
-                nc.vector.tensor_scalar_min(out=chain[i][:], in0=chain[i][:], scalar1=TANH_CAP)
-        quantise_w(W_CHUNKS - 1)
+        def cap(bt):
+            nc.vector.tensor_scalar_min(out=chain[bt][:], in0=chain[bt][:], scalar1=TANH_CAP)
 
-        for bt in range(B_TILES):
+        def softplus(bt):
             nc.scalar.activation(
                 out=chain[bt][:], in_=chain[bt][:], func=ACT.Ln, scale=-0.5, bias=half[:]
             )
 
         dz_codes = [keep.tile([P, PASSES * P], U32, name="dz_codes%d" % bt, align_bytes=64) for bt in range(B_TILES)]
         dz_scales = [keep.tile([P, PASSES * P], U8, name="dz_scales%d" % bt, align_bytes=64) for bt in range(B_TILES)]
+        units = [(bt, c, 2) for bt in range(B_TILES - 1) for c in (0, 2)] + [(3, 0, 2), (3, 2, 1), (3, 3, 1)]
         work = {}
         grad_t = {}
         dz_grouped = {}
         acc = {}
 
-        def part(tiles, s):
-            bt, hc = divmod(s, PASSES // PAIR)
-            return tiles[bt][:, hc * PAIR : (hc + 1) * PAIR]
+        def k_cols(u):
+            return slice(units[u][1] * K_PASS, (units[u][1] + units[u][2]) * K_PASS)
 
-        def ratio(s):
-            nc.scalar.activation(out=part(chain, s), in_=part(chain, s), func=ACT.Sigmoid, scale=-2.0)
+        def word_cols(u):
+            return slice(units[u][1] * P, (units[u][1] + units[u][2]) * P)
 
-        def transpose_grad(s):
-            bt, hc = divmod(s, PASSES // PAIR)
-            grad_t[s] = psum_t.tile([P, PACK, PAIR * P], BF16, name="grad_t", tag="transposed")
-            for cc in range(PAIR):
+        def ratio(u):
+            view = chain[units[u][0]][:, k_cols(u)]
+            nc.scalar.activation(out=view, in_=view, func=ACT.Sigmoid, scale=-2.0)
+
+        def turn_grad(u):
+            bt, c0, n = units[u]
+            grad_t[u] = psum_t.tile([P, PACK, n * P], BF16, name="grad_t", tag="transposed")
+            for c in range(n):
                 for t in range(PACK):
-                    k0 = (hc * PAIR + cc) * K_PASS + t * P
+                    k0 = (c0 + c) * K_PASS + t * P
                     nc.tensor.matmul(
-                        grad_t[s][:, t, cc * P : (cc + 1) * P], lhsT=grad[bt][:, k0 : k0 + P], rhs=minus_four[:],
+                        grad_t[u][:, t, c * P : (c + 1) * P], lhsT=grad[bt][:, k0 : k0 + P], rhs=minus_four[:],
                         start=True, stop=True,
                     )
 
-        def slope_term(s):
-            work[s] = u_pool.tile([P, PAIR, P, PACK], F32, name="work")
+        def first_factor(u):
+            bt, c0, n = units[u]
+            work[u] = u_pool.tile([P, n * K_PASS], F32, name="work")
             nc.vector.scalar_tensor_tensor(
-                out=work[s][:].rearrange("p c b t -> p (c b t)"),
-                in0=part(chain, s).rearrange("p c b t -> p (c b t)"),
-                scalar=1.0,
-                in1=part(silu, s).rearrange("p c b t -> p (c b t)"),
+                out=work[u][:], in0=chain[bt][:, k_cols(u)], scalar=1.0, in1=silu[bt][:, k_cols(u)],
                 op0=ALU.subtract, op1=ALU.mult,
             )
 
-        def derivative(s):
+        def product(u):
             nc.vector.scalar_tensor_tensor(
-                out=work[s][:].rearrange("p c b t -> p (c b t)"),
-                in0=work[s][:].rearrange("p c b t -> p (c b t)"),
-                scalar=0.5,
-                in1=part(chain, s).rearrange("p c b t -> p (c b t)"),
+                out=work[u][:], in0=work[u][:], scalar=0.5, in1=chain[units[u][0]][:, k_cols(u)],
                 op0=ALU.subtract, op1=ALU.mult,
             )
 
-        def times_grad(s):
-            dz_grouped[s] = dz_pool.tile([P, PAIR * P, PACK], BF16, name="dz_grouped", align_bytes=64)
+        def times_grad(u):
+            dz_grouped[u] = dz_pool.tile([P, units[u][2] * P, PACK], BF16, name="dz_grouped", align_bytes=64)
             nc.vector.scalar_tensor_tensor(
-                out=dz_grouped[s][:],
-                in0=work[s][:].rearrange("p c b t -> p (c b) t"),
+                out=dz_grouped[u][:],
+                in0=work[u][:].rearrange("p (x t) -> p x t", t=PACK),
                 scalar=0.25,
-                in1=grad_t[s][:].rearrange("p t x -> p x t"),
+                in1=grad_t[u][:].rearrange("p t x -> p x t"),
                 op0=ALU.add,
                 op1=ALU.mult,
             )
 
-        def quantise_dz(s):
-            bt, hc = divmod(s, PASSES // PAIR)
-            cols = slice(hc * PAIR * P, (hc + 1) * PAIR * P)
+        def quantise_dz(u):
+            bt = units[u][0]
             nc.vector.quantize_mx(
-                out=dz_codes[bt][:, cols].bitcast(E5M2_X4),
-                scales=dz_scales[bt][:, cols],
-                in_=dz_grouped[s][:].rearrange("p x t -> p (x t)"),
+                out=dz_codes[bt][:, word_cols(u)].bitcast(E5M2_X4),
+                scales=dz_scales[bt][:, word_cols(u)],
+                in_=dz_grouped[u][:].rearrange("p x t -> p (x t)"),
             )
 
-        def multiply(s):
-            bt, hc = divmod(s, PASSES // PAIR)
-            for j in range(N_TILES):
-                if hc == 0:
-                    acc[bt, j] = psum_o.tile([P, N_TILE], F32, name="acc")
-                for c in range(hc * PAIR, (hc + 1) * PAIR):
-                    nc.tensor.matmul_mx(
-                        out=acc[bt, j][:],
-                        lhsT=dz_codes[bt][:, c * P : (c + 1) * P].bitcast(E5M2_X4),
-                        lhsT_scale=dz_scales[bt][:, c * P : (c + 1) * P],
-                        rhs=w_codes[c][:, j * N_TILE : (j + 1) * N_TILE].bitcast(E4M3_X4),
-                        rhs_scale=w_scales[c][:, j * N_TILE : (j + 1) * N_TILE],
-                        start=(c == 0),
-                        stop=(c == PASSES - 1),
-                    )
+        def multiply(bt, c, j):
+            if c == 0:
+                acc[bt, j] = psum_o.tile([P, N_TILE], F32, name="acc")
+            nc.tensor.matmul_mx(
+                out=acc[bt, j][:],
+                lhsT=dz_codes[bt][:, c * P : (c + 1) * P].bitcast(E5M2_X4),
+                lhsT_scale=dz_scales[bt][:, c * P : (c + 1) * P],
+                rhs=w_codes[c][:, j * N_TILE : (j + 1) * N_TILE].bitcast(E4M3_X4),
+                rhs_scale=w_scales[c][:, j * N_TILE : (j + 1) * N_TILE],
+                start=(c == 0),
+                stop=(c == PASSES - 1),
+            )
+
+        def multiply_unit(u, tiles):
+            bt, c0, n = units[u]
+            for j in tiles:
+                for c in range(c0, c0 + n):
+                    multiply(bt, c, j)
+
+        def store(bt, j, copy):
+            o_sb = o_pool.tile([P, N_TILE], F32, name="o_sb")
+            copy(out=o_sb[:], in_=acc[bt, j][:])
+            nc.sync.dma_start(out=out[rows(bt), j * N_TILE : (j + 1) * N_TILE], in_=o_sb[:])
 
         def store_rows(bt):
             for j in range(N_TILES):
-                o_sb = o_pool.tile([P, N_TILE], F32, name="o_sb")
-                nc.scalar.copy(out=o_sb[:], in_=acc[bt, j][:])
-                nc.sync.dma_start(out=out[rows(bt), j * N_TILE : (j + 1) * N_TILE], in_=o_sb[:])
+                store(bt, j, nc.scalar.copy)
 
-        for step in range(UNITS + AHEAD + 1):
-            front = step - AHEAD
-            back = front - 1
-            if step < UNITS:
-                ratio(step)
-            if 0 <= front + 1 < UNITS:
-                transpose_grad(front + 1)
-            if 0 <= front < UNITS:
-                slope_term(front)
-            if 0 <= back:
-                times_grad(back)
-            if 0 <= front < UNITS:
-                derivative(front)
-            if 0 <= back:
-                quantise_dz(back)
-                multiply(back)
-                if back % (PASSES // PAIR) == PASSES // PAIR - 1:
-                    store_rows(back // (PASSES // PAIR))
+        LATE = [8]
+        for i in range(B_TILES * PASSES):
+            z_functions(i)
+        early = [i for i in range(len(w_pieces)) if i not in LATE]
+        cap_after = {3: 0, 4: 1, 6: 2, 7: 3}
+        for i in early:
+            regroup_w(i, nc.vector.tensor_copy)
+            if i > 0:
+                quantise_w(i - 1)
+            if i in cap_after:
+                cap(cap_after[i])
+        quantise_w(early[-1])
+
+        softplus(0)
+        softplus(1)
+        for u in range(4):
+            ratio(u)
+        for i in LATE:
+            regroup_w(i, nc.scalar.copy)
+        softplus(2)
+        softplus(3)
+        ratio(4)
+
+        ALL_TILES = range(N_TILES)
+        turn_grad(0)
+        for u in range(len(units)):
+            if u + 1 < len(units):
+                turn_grad(u + 1)
+            first_factor(u)
+            if u > 0:
+                times_grad(u - 1)
+            if u == 3:
+                for i in LATE:
+                    quantise_w(i)
+                multiply_unit(1, [2, 3])
+                store_rows(0)
+            product(u)
+            if u > 0:
+                quantise_dz(u - 1)
+                multiply_unit(u - 1, [0, 1] if u - 1 == 1 else ALL_TILES)
+            if u == 3:
+                ratio(5)
+                ratio(6)
+            if u == 4:
+                store_rows(1)
+                for v in range(7, len(units)):
+                    ratio(v)
+            if u == 6:
+                store_rows(2)
+        times_grad(len(units) - 1)
+        quantise_dz(len(units) - 1)
+        for j in ALL_TILES:
+            multiply_unit(len(units) - 1, [j])
+            store(B_TILES - 1, j, nc.vector.tensor_copy if j % 2 else nc.scalar.copy)

@@ -21,8 +21,7 @@ B_TILES = BATCH // P
 PASSES = DR // K_PASS
 N_TILE = 512
 N_TILES = DR // N_TILE
-HALF_W = 1024
-TANH_CAP = 1.0 - 2.0**-24
+TINY = 2.0**-100
 
 FLOPS = 2 * BATCH * DR * DR
 BYTES = 2 * DR * DR + (4 + 2 + 4) * BATCH * DR
@@ -34,14 +33,14 @@ def tile_gnn_layer_pa_v_kernel(
     nc = tc.nc
     with ExitStack() as stack:
         keep = stack.enter_context(tc.tile_pool(name="keep", bufs=1))
-        z_pool = stack.enter_context(tc.tile_pool(name="z_pool", bufs=8))
-        w_pool = stack.enter_context(tc.tile_pool(name="w_pool", bufs=3))
-        wg_pool = stack.enter_context(tc.tile_pool(name="wg_pool", bufs=2))
+        z_pool = stack.enter_context(tc.tile_pool(name="z_pool", bufs=9))
+        w_pool = stack.enter_context(tc.tile_pool(name="w_pool", bufs=6))
+        wg_pool = stack.enter_context(tc.tile_pool(name="wg_pool", bufs=3))
         u_pool = stack.enter_context(tc.tile_pool(name="u_pool", bufs=3))
         dz_pool = stack.enter_context(tc.tile_pool(name="dz_pool", bufs=2))
         o_pool = stack.enter_context(tc.tile_pool(name="o_pool", bufs=4))
-        psum_t = stack.enter_context(tc.psum_pool(name="psum_t", bufs=2))
-        psum_o = stack.enter_context(tc.psum_pool(name="psum_o", bufs=6))
+        psum = stack.enter_context(tc.psum_pool(name="psum", bufs=6))
+        psum_g = stack.enter_context(tc.psum_pool(name="psum_g", bufs=2))
         stack.enter_context(tc.manual_schedule())
 
         ident_f32 = keep.tile([P, P], F32, name="ident_f32")
@@ -50,12 +49,14 @@ def tile_gnn_layer_pa_v_kernel(
         nc.vector.tensor_scalar_mul(out=minus_four[:], in0=ident_f32[:], scalar1=-4.0)
         half = keep.tile([P, 1], F32, name="half")
         nc.vector.memset(half[:], 0.5)
+        tiny = keep.tile([P, 1], F32, name="tiny")
+        nc.vector.memset(tiny[:], TINY)
 
         def rows(bt):
             return slice(bt * P, (bt + 1) * P)
 
-        w_pieces = [(0, 0, 512), (0, 512, 512), (0, HALF_W, HALF_W)]
-        w_pieces += [(c, h * HALF_W, HALF_W) for c in range(1, PASSES) for h in range(2)]
+        w_pieces = [(0, 0, 256), (0, 256, 256)] + [(0, n, 512) for n in (512, 1024, 1536)]
+        w_pieces += [(c, n, 512) for c in range(1, PASSES) for n in range(0, DR, 512)]
         w_raw = []
         z_piece = []
 
@@ -70,46 +71,63 @@ def tile_gnn_layer_pa_v_kernel(
             )
             w_raw.append(raw)
 
-        def load_z():
+        def load_z(pieces):
             bt, c = divmod(len(z_piece), PASSES)
-            piece = z_pool.tile([P, K_PASS], F32, name="z_piece")
-            nc.sync.dma_start(out=piece[:], in_=z_rf[rows(bt), c * K_PASS : (c + 1) * K_PASS])
-            z_piece.append(piece)
+            raw = z_pool.tile([P, pieces * K_PASS], F32, name="z_raw")
+            nc.sync.dma_start(out=raw[:], in_=z_rf[rows(bt), c * K_PASS : (c + pieces) * K_PASS])
+            for i in range(pieces):
+                z_piece.append(raw[:, i * K_PASS : (i + 1) * K_PASS])
 
-        for kind in "zwzwzzwzzzwzzzwzzzwzzzwww":
-            if kind == "z":
-                load_z()
-            else:
-                load_w()
         grad = []
-        for bt in range(B_TILES):
-            grad.append(keep.tile([P, DR], BF16, name="grad%d" % bt))
-            nc.sync.dma_start(out=grad[bt][:], in_=grad_out[rows(bt), :])
+
+        def load_grad():
+            tile = keep.tile([P, DR], BF16, name="grad%d" % len(grad))
+            nc.sync.dma_start(out=tile[:], in_=grad_out[rows(len(grad)), :])
+            grad.append(tile)
+
+        for kind in "wzwzwZwwZwwZZwwZwwZZwwwwwwgggg":
+            if kind == "z":
+                load_z(1)
+            elif kind == "Z":
+                load_z(2)
+            elif kind == "w":
+                load_w()
+            else:
+                load_grad()
 
         silu = [keep.tile([P, PASSES * P * PACK], F32, name="silu%d" % bt) for bt in range(B_TILES)]
         chain = [keep.tile([P, PASSES * P * PACK], F32, name="chain%d" % bt) for bt in range(B_TILES)]
+        z_t = {}
 
-        def z_functions(i):
-            bt, c = divmod(i, PASSES)
-            cols = slice(c * K_PASS, (c + 1) * K_PASS)
-            z_t = psum_t.tile([P, PACK, P], F32, name="z_t", tag="transposed")
+        def turn_z(i):
+            z_t[i] = psum.tile([P, PACK, P], F32, name="z_t", tag="bank")
             for t in range(PACK):
-                nc.tensor.transpose(z_t[:, t, :], z_piece[i][:, t * P : (t + 1) * P], ident_f32[:])
-            z_words = z_t[:].rearrange("p t b -> p b t")
-            for dest, func, scale in ((silu, ACT.Silu, 1.0), (chain, ACT.Tanh, 0.5)):
-                nc.scalar.activation(
-                    out=dest[bt][:, cols].rearrange("p (b t) -> p b t", t=PACK),
-                    in_=z_words, func=func, scale=scale,
-                )
+                nc.tensor.transpose(z_t[i][:, t, :], z_piece[i][:, t * P : (t + 1) * P], ident_f32[:])
+
+        def z_function(i, dest, func, scale):
+            bt, c = divmod(i, PASSES)
+            nc.scalar.activation(
+                out=dest[bt][:, c * K_PASS : (c + 1) * K_PASS].rearrange("p (b t) -> p b t", t=PACK),
+                in_=z_t[i][:].rearrange("p t b -> p b t"), func=func, scale=scale,
+            )
+
+        def silu_of(i):
+            z_function(i, silu, ACT.Silu, 1.0)
+
+        def tanh_of(i):
+            z_function(i, chain, ACT.Tanh, 0.5)
+
+        def q_of(i):
+            z_function(i, chain, ACT.Sigmoid, -1.0)
 
         w_codes = [keep.tile([P, DR], U32, name="w_codes%d" % c, align_bytes=64) for c in range(PASSES)]
         w_scales = [keep.tile([P, DR], U8, name="w_scales%d" % c, align_bytes=64) for c in range(PASSES)]
         w_grouped = {}
 
-        def regroup_w(i, copy):
+        def regroup_w(i):
             width = w_pieces[i][2]
             w_grouped[i] = wg_pool.tile([P, width, PACK], BF16, name="w_grouped", align_bytes=64)
-            copy(
+            nc.vector.tensor_copy(
                 out=w_grouped[i][:].rearrange("p (q i) t -> p q t i", i=4),
                 in_=w_raw[i][:].rearrange("p t (q i) -> p q t i", i=4),
             )
@@ -122,35 +140,36 @@ def tile_gnn_layer_pa_v_kernel(
                 in_=w_grouped[i][:].rearrange("p n t -> p (n t)"),
             )
 
-        def cap(bt):
-            nc.vector.tensor_scalar_min(out=chain[bt][:], in0=chain[bt][:], scalar1=TANH_CAP)
+        def k_cols(c0, n):
+            return slice(c0 * K_PASS, (c0 + n) * K_PASS)
 
-        def softplus(bt):
-            nc.scalar.activation(
-                out=chain[bt][:], in_=chain[bt][:], func=ACT.Ln, scale=-0.5, bias=half[:]
-            )
+        def square_of(bt, c0, n):
+            view = chain[bt][:, k_cols(c0, n)]
+            nc.scalar.activation(out=view, in_=view, func=ACT.Square, scale=-0.5, bias=half[:])
+
+        def ln_of_q(bt, c0, n):
+            view = chain[bt][:, k_cols(c0, n)]
+            nc.scalar.activation(out=view, in_=view, func=ACT.Ln, bias=tiny[:])
 
         dz_codes = [keep.tile([P, PASSES * P], U32, name="dz_codes%d" % bt, align_bytes=64) for bt in range(B_TILES)]
         dz_scales = [keep.tile([P, PASSES * P], U8, name="dz_scales%d" % bt, align_bytes=64) for bt in range(B_TILES)]
-        units = [(bt, c, 2) for bt in range(B_TILES - 1) for c in (0, 2)] + [(3, 0, 2), (3, 2, 1), (3, 3, 1)]
+        units = [(bt, c, 2) for bt in range(3) for c in (0, 2)] + [(3, c, 1) for c in range(4)]
         work = {}
         grad_t = {}
         dz_grouped = {}
         acc = {}
 
-        def k_cols(u):
-            return slice(units[u][1] * K_PASS, (units[u][1] + units[u][2]) * K_PASS)
-
-        def word_cols(u):
-            return slice(units[u][1] * P, (units[u][1] + units[u][2]) * P)
-
         def ratio(u):
-            view = chain[units[u][0]][:, k_cols(u)]
-            nc.scalar.activation(out=view, in_=view, func=ACT.Sigmoid, scale=-2.0)
+            bt, c0, n = units[u]
+            view = chain[bt][:, k_cols(c0, n)]
+            nc.scalar.activation(out=view, in_=view, func=ACT.Sigmoid, scale=-1.0 if u < 5 else -2.0)
+
+        def ln_unit(u):
+            ln_of_q(*units[u])
 
         def turn_grad(u):
             bt, c0, n = units[u]
-            grad_t[u] = psum_t.tile([P, PACK, n * P], BF16, name="grad_t", tag="transposed")
+            grad_t[u] = psum_g.tile([P, PACK, n * P], BF16, name="grad_t")
             for c in range(n):
                 for t in range(PACK):
                     k0 = (c0 + c) * K_PASS + t * P
@@ -163,13 +182,14 @@ def tile_gnn_layer_pa_v_kernel(
             bt, c0, n = units[u]
             work[u] = u_pool.tile([P, n * K_PASS], F32, name="work")
             nc.vector.scalar_tensor_tensor(
-                out=work[u][:], in0=chain[bt][:, k_cols(u)], scalar=1.0, in1=silu[bt][:, k_cols(u)],
+                out=work[u][:], in0=chain[bt][:, k_cols(c0, n)], scalar=1.0, in1=silu[bt][:, k_cols(c0, n)],
                 op0=ALU.subtract, op1=ALU.mult,
             )
 
         def product(u):
+            bt, c0, n = units[u]
             nc.vector.scalar_tensor_tensor(
-                out=work[u][:], in0=work[u][:], scalar=0.5, in1=chain[units[u][0]][:, k_cols(u)],
+                out=work[u][:], in0=work[u][:], scalar=0.5, in1=chain[bt][:, k_cols(c0, n)],
                 op0=ALU.subtract, op1=ALU.mult,
             )
 
@@ -185,16 +205,17 @@ def tile_gnn_layer_pa_v_kernel(
             )
 
         def quantise_dz(u):
-            bt = units[u][0]
+            bt, c0, n = units[u]
+            cols = slice(c0 * P, (c0 + n) * P)
             nc.vector.quantize_mx(
-                out=dz_codes[bt][:, word_cols(u)].bitcast(E5M2_X4),
-                scales=dz_scales[bt][:, word_cols(u)],
+                out=dz_codes[bt][:, cols].bitcast(E5M2_X4),
+                scales=dz_scales[bt][:, cols],
                 in_=dz_grouped[u][:].rearrange("p x t -> p (x t)"),
             )
 
         def multiply(bt, c, j):
             if c == 0:
-                acc[bt, j] = psum_o.tile([P, N_TILE], F32, name="acc")
+                acc[bt, j] = psum.tile([P, N_TILE], F32, name="acc", tag="bank")
             nc.tensor.matmul_mx(
                 out=acc[bt, j][:],
                 lhsT=dz_codes[bt][:, c * P : (c + 1) * P].bitcast(E5M2_X4),
@@ -220,57 +241,53 @@ def tile_gnn_layer_pa_v_kernel(
             for j in range(N_TILES):
                 store(bt, j, nc.scalar.copy)
 
-        LATE = [8]
+        ALL_TILES = range(N_TILES)
+        HEAD = 10
         for i in range(B_TILES * PASSES):
-            z_functions(i)
-        early = [i for i in range(len(w_pieces)) if i not in LATE]
-        cap_after = {3: 0, 4: 1, 6: 2, 7: 3}
-        for i in early:
-            regroup_w(i, nc.vector.tensor_copy)
+            turn_z(i)
+            silu_of(i)
+            if i < HEAD:
+                tanh_of(i)
+            if i < HEAD and i % 2 == 1:
+                square_of(i // PASSES, i % PASSES - 1, 2)
+        for i in range(len(w_pieces)):
+            regroup_w(i)
             if i > 0:
                 quantise_w(i - 1)
-            if i in cap_after:
-                cap(cap_after[i])
-        quantise_w(early[-1])
-
-        softplus(0)
-        softplus(1)
-        for u in range(4):
+        for u in range(5):
+            ln_unit(u)
+        for u in range(5):
             ratio(u)
-        for i in LATE:
-            regroup_w(i, nc.scalar.copy)
-        softplus(2)
-        softplus(3)
-        ratio(4)
-
-        ALL_TILES = range(N_TILES)
         turn_grad(0)
+        turn_grad(1)
+        for i in range(HEAD, B_TILES * PASSES):
+            turn_z(i)
+            q_of(i)
+        for u in range(5, 6):
+            ln_unit(u)
+        ln_of_q(3, 0, PASSES)
+        for u in range(5, 6):
+            ratio(u)
+        LAST = len(units) - 1
         for u in range(len(units)):
-            if u + 1 < len(units):
-                turn_grad(u + 1)
             first_factor(u)
-            if u > 0:
+            if u == 0:
+                quantise_w(len(w_pieces) - 1)
+            else:
                 times_grad(u - 1)
-            if u == 3:
-                for i in LATE:
-                    quantise_w(i)
-                multiply_unit(1, [2, 3])
-                store_rows(0)
+                if u + 1 <= LAST:
+                    turn_grad(u + 1)
             product(u)
             if u > 0:
                 quantise_dz(u - 1)
-                multiply_unit(u - 1, [0, 1] if u - 1 == 1 else ALL_TILES)
-            if u == 3:
-                ratio(5)
-                ratio(6)
-            if u == 4:
-                store_rows(1)
-                for v in range(7, len(units)):
-                    ratio(v)
-            if u == 6:
-                store_rows(2)
-        times_grad(len(units) - 1)
-        quantise_dz(len(units) - 1)
+                multiply_unit(u - 1, ALL_TILES)
+                if u == 4:
+                    for v in range(6, len(units)):
+                        ratio(v)
+                if units[u][0] > units[u - 1][0]:
+                    store_rows(units[u - 1][0])
+        times_grad(LAST)
+        quantise_dz(LAST)
         for j in ALL_TILES:
-            multiply_unit(len(units) - 1, [j])
+            multiply_unit(LAST, [j])
             store(B_TILES - 1, j, nc.vector.tensor_copy if j % 2 else nc.scalar.copy)

@@ -33,8 +33,8 @@ def tile_gnn_layer_pa_v_kernel(
     nc = tc.nc
     with ExitStack() as stack:
         keep = stack.enter_context(tc.tile_pool(name="keep", bufs=1))
-        z_pool = stack.enter_context(tc.tile_pool(name="z_pool", bufs=9))
-        w_pool = stack.enter_context(tc.tile_pool(name="w_pool", bufs=6))
+        z_pool = stack.enter_context(tc.tile_pool(name="z_pool", bufs=8))
+        w_pool = stack.enter_context(tc.tile_pool(name="w_pool", bufs=3))
         wg_pool = stack.enter_context(tc.tile_pool(name="wg_pool", bufs=3))
         u_pool = stack.enter_context(tc.tile_pool(name="u_pool", bufs=3))
         dz_pool = stack.enter_context(tc.tile_pool(name="dz_pool", bufs=2))
@@ -55,8 +55,8 @@ def tile_gnn_layer_pa_v_kernel(
         def rows(bt):
             return slice(bt * P, (bt + 1) * P)
 
-        w_pieces = [(0, 0, 256), (0, 256, 256)] + [(0, n, 512) for n in (512, 1024, 1536)]
-        w_pieces += [(c, n, 512) for c in range(1, PASSES) for n in range(0, DR, 512)]
+        w_pieces = [(0, 0, 256), (0, 256, 256), (0, 512, 512), (0, 1024, 1024)]
+        w_pieces += [(c, n, 1024) for c in range(1, PASSES) for n in (0, 1024)]
         w_raw = []
         z_piece = []
 
@@ -85,7 +85,7 @@ def tile_gnn_layer_pa_v_kernel(
             nc.sync.dma_start(out=tile[:], in_=grad_out[rows(len(grad)), :])
             grad.append(tile)
 
-        for kind in "wzwzwZwwZwwZZwwZwwZZwwwwwwgggg":
+        for kind in "wzwzwZwZwZZwZwZZwwwgggg":
             if kind == "z":
                 load_z(1)
             elif kind == "Z":

@@ -162,10 +162,21 @@ def tile_gnn_layer_pa_v_kernel(
         def ratio(u):
             bt, c0, n = units[u]
             view = chain[bt][:, k_cols(c0, n)]
-            nc.scalar.activation(out=view, in_=view, func=ACT.Sigmoid, scale=-1.0 if u < 5 else -2.0)
+            nc.scalar.activation(out=view, in_=view, func=ACT.Sigmoid, scale=-1.0 if u < 5 and u not in CAPPED else -2.0)
+
+        CAPPED = {1:3,3:5}
+
+        def cap(bt, c0, n):
+            view = chain[bt][:, k_cols(c0, n)]
+            nc.vector.tensor_scalar_min(out=view, in0=view, scalar1=1.0 - 2.0**-24)
 
         def ln_unit(u):
-            ln_of_q(*units[u])
+            if u in CAPPED:
+                bt, c0, n = units[u]
+                view = chain[bt][:, k_cols(c0, n)]
+                nc.scalar.activation(out=view, in_=view, func=ACT.Ln, scale=-0.5, bias=half[:])
+            else:
+                ln_of_q(*units[u])
 
         def turn_grad(u):
             bt, c0, n = units[u]
@@ -248,12 +259,14 @@ def tile_gnn_layer_pa_v_kernel(
             silu_of(i)
             if i < HEAD:
                 tanh_of(i)
-            if i < HEAD and i % 2 == 1:
+            if i < HEAD and i % 2 == 1 and i // 2 not in CAPPED:
                 square_of(i // PASSES, i % PASSES - 1, 2)
         for i in range(len(w_pieces)):
             regroup_w(i)
             if i > 0:
                 quantise_w(i - 1)
+            if i in CAPPED.values():
+                cap(*units[[u for u in CAPPED if CAPPED[u] == i][0]])
         for u in range(5):
             ln_unit(u)
         for u in range(5):

@@ -56,7 +56,7 @@ def tile_gnn_layer_pa_v_kernel(
             return slice(bt * P, (bt + 1) * P)
 
         w_pieces = [(0, 0, 256), (0, 256, 256), (0, 512, 512), (0, 1024, 1024)]
-        w_pieces += [(c, n, 1024) for c in range(1, PASSES) for n in (0, 1024)]
+        w_pieces += [(c, n, 1024) for c in (1, 2) for n in (0, 1024)] + [(3, 0, 1024), (3, 1024, 512), (3, 1536, 512)]
         w_raw = []
         z_piece = []
 
@@ -85,7 +85,7 @@ def tile_gnn_layer_pa_v_kernel(
             nc.sync.dma_start(out=tile[:], in_=grad_out[rows(len(grad)), :])
             grad.append(tile)
 
-        for kind in "wzwzwZwZwZZwZwZZwwwgggg":
+        for kind in "wzwzwZwZwZZwZwZZwwwwgggg":
             if kind == "z":
                 load_z(1)
             elif kind == "Z":
@@ -124,10 +124,10 @@ def tile_gnn_layer_pa_v_kernel(
         w_scales = [keep.tile([P, DR], U8, name="w_scales%d" % c, align_bytes=64) for c in range(PASSES)]
         w_grouped = {}
 
-        def regroup_w(i):
+        def regroup_w(i, copy):
             width = w_pieces[i][2]
             w_grouped[i] = wg_pool.tile([P, width, PACK], BF16, name="w_grouped", align_bytes=64)
-            nc.vector.tensor_copy(
+            copy(
                 out=w_grouped[i][:].rearrange("p (q i) t -> p q t i", i=4),
                 in_=w_raw[i][:].rearrange("p t (q i) -> p q t i", i=4),
             )
@@ -261,8 +261,9 @@ def tile_gnn_layer_pa_v_kernel(
                 tanh_of(i)
             if i < HEAD and i % 2 == 1 and i // 2 not in CAPPED:
                 square_of(i // PASSES, i % PASSES - 1, 2)
-        for i in range(len(w_pieces)):
-            regroup_w(i)
+        LATE_W = len(w_pieces) - 1
+        for i in range(LATE_W):
+            regroup_w(i, nc.vector.tensor_copy)
             if i > 0:
                 quantise_w(i - 1)
             if i in CAPPED.values():
@@ -271,6 +272,8 @@ def tile_gnn_layer_pa_v_kernel(
             ln_unit(u)
         for u in range(5):
             ratio(u)
+            if u == 1:
+                regroup_w(LATE_W, nc.scalar.copy)
         turn_grad(0)
         turn_grad(1)
         for i in range(HEAD, B_TILES * PASSES):
@@ -284,8 +287,10 @@ def tile_gnn_layer_pa_v_kernel(
         LAST = len(units) - 1
         for u in range(len(units)):
             first_factor(u)
+            if u == 2:
+                quantise_w(LATE_W)
             if u == 0:
-                quantise_w(len(w_pieces) - 1)
+                quantise_w(LATE_W - 1)
             else:
                 times_grad(u - 1)
                 if u + 1 <= LAST:
@@ -293,7 +298,14 @@ def tile_gnn_layer_pa_v_kernel(
             product(u)
             if u > 0:
                 quantise_dz(u - 1)
-                multiply_unit(u - 1, ALL_TILES)
+                if u == 3:
+                    multiply_unit(2, [0, 1])
+                elif u == 4:
+                    multiply_unit(3, [0, 1])
+                    multiply_unit(2, [2, 3])
+                    multiply_unit(3, [2, 3])
+                else:
+                    multiply_unit(u - 1, ALL_TILES)
                 if u == 4:
                     for v in range(6, len(units)):
                         ratio(v)

@@ -164,7 +164,7 @@ def tile_gnn_layer_pa_v_kernel(
             view = chain[bt][:, k_cols(c0, n)]
             nc.scalar.activation(out=view, in_=view, func=ACT.Sigmoid, scale=-1.0 if u < 5 and u not in CAPPED else -2.0)
 
-        CAPPED = {1:3,3:5}
+        CAPPED = {3:5,4:6}
 
         def cap(bt, c0, n):
             view = chain[bt][:, k_cols(c0, n)]
@@ -272,8 +272,8 @@ def tile_gnn_layer_pa_v_kernel(
             ln_unit(u)
         for u in range(5):
             ratio(u)
-            if u == 1:
-                regroup_w(LATE_W, nc.scalar.copy)
+            if u in [1]:
+                regroup_w(LATE_W + [1].index(u), nc.scalar.copy)
         turn_grad(0)
         turn_grad(1)
         for i in range(HEAD, B_TILES * PASSES):
@@ -287,8 +287,8 @@ def tile_gnn_layer_pa_v_kernel(
         LAST = len(units) - 1
         for u in range(len(units)):
             first_factor(u)
-            if u == 2:
-                quantise_w(LATE_W)
+            if u in [2]:
+                quantise_w(LATE_W + [2].index(u))
             if u == 0:
                 quantise_w(LATE_W - 1)
             else:

from contextlib import ExitStack

import concourse.mybir as mybir
from concourse.masks import make_identity

F32 = mybir.dt.float32
BF16 = mybir.dt.bfloat16
U32 = mybir.dt.uint32
U8 = mybir.dt.uint8
E4M3_X4 = mybir.dt.float8_e4m3fn_x4
E5M2_X4 = mybir.dt.float8_e5m2_x4
ACT = mybir.ActivationFunctionType
ALU = mybir.AluOpType

P = 128
PACK = 4
K_PASS = P * PACK
BATCH = 512
DR = 2048
B_TILES = BATCH // P
PASSES = DR // K_PASS
N_TILE = 512
N_TILES = DR // N_TILE
TINY = 2.0**-100

FLOPS = 2 * BATCH * DR * DR
BYTES = 2 * DR * DR + (4 + 2 + 4) * BATCH * DR


def tile_gnn_layer_pa_v_kernel(
    tc, BB_feature, RF_feature, W_rfrf, b_rfrf, W_bbrf, b_bbrf, z_rf, grad_out, out
):
    nc = tc.nc
    with ExitStack() as stack:
        keep = stack.enter_context(tc.tile_pool(name="keep", bufs=1))
        z_pool = stack.enter_context(tc.tile_pool(name="z_pool", bufs=8))
        w_pool = stack.enter_context(tc.tile_pool(name="w_pool", bufs=3))
        wg_pool = stack.enter_context(tc.tile_pool(name="wg_pool", bufs=3))
        u_pool = stack.enter_context(tc.tile_pool(name="u_pool", bufs=3))
        dz_pool = stack.enter_context(tc.tile_pool(name="dz_pool", bufs=2))
        o_pool = stack.enter_context(tc.tile_pool(name="o_pool", bufs=4))
        psum = stack.enter_context(tc.psum_pool(name="psum", bufs=6))
        psum_g = stack.enter_context(tc.psum_pool(name="psum_g", bufs=2))
        stack.enter_context(tc.manual_schedule())

        ident_f32 = keep.tile([P, P], F32, name="ident_f32")
        make_identity(nc, ident_f32[:])
        minus_four = keep.tile([P, P], BF16, name="minus_four")
        nc.vector.tensor_scalar_mul(out=minus_four[:], in0=ident_f32[:], scalar1=-4.0)
        half = keep.tile([P, 1], F32, name="half")
        nc.vector.memset(half[:], 0.5)
        tiny = keep.tile([P, 1], F32, name="tiny")
        nc.vector.memset(tiny[:], TINY)

        def rows(bt):
            return slice(bt * P, (bt + 1) * P)

        w_pieces = [(0, 0, 256), (0, 256, 256), (0, 512, 512), (0, 1024, 1024)]
        w_pieces += [(c, n, 1024) for c in (1, 2) for n in (0, 1024)] + [(3, 0, 1024), (3, 1024, 512), (3, 1536, 512)]
        w_raw = []
        z_piece = []

        def load_w():
            c, n0, width = w_pieces[len(w_raw)]
            raw = w_pool.tile([P, PACK, width], BF16, name="w_raw")
            nc.sync.dma_start(
                out=raw[:],
                in_=W_rfrf[c * K_PASS : (c + 1) * K_PASS, n0 : n0 + width].rearrange(
                    "(t p) n -> p t n", p=P
                ),
            )
            w_raw.append(raw)

        def load_z(pieces):
            bt, c = divmod(len(z_piece), PASSES)
            raw = z_pool.tile([P, pieces * K_PASS], F32, name="z_raw")
            nc.sync.dma_start(out=raw[:], in_=z_rf[rows(bt), c * K_PASS : (c + pieces) * K_PASS])
            for i in range(pieces):
                z_piece.append(raw[:, i * K_PASS : (i + 1) * K_PASS])

        grad = []

        def load_grad():
            tile = keep.tile([P, DR], BF16, name="grad%d" % len(grad))
            nc.sync.dma_start(out=tile[:], in_=grad_out[rows(len(grad)), :])
            grad.append(tile)

        for kind in "wzwzwZwZwZZwZwZZwwwwgggg":
            if kind == "z":
                load_z(1)
            elif kind == "Z":
                load_z(2)
            elif kind == "w":
                load_w()
            else:
                load_grad()

        silu = [keep.tile([P, PASSES * P * PACK], F32, name="silu%d" % bt) for bt in range(B_TILES)]
        chain = [keep.tile([P, PASSES * P * PACK], F32, name="chain%d" % bt) for bt in range(B_TILES)]
        z_t = {}

        def turn_z(i):
            z_t[i] = psum.tile([P, PACK, P], F32, name="z_t", tag="bank")
            for t in range(PACK):
                nc.tensor.transpose(z_t[i][:, t, :], z_piece[i][:, t * P : (t + 1) * P], ident_f32[:])

        def z_function(i, dest, func, scale):
            bt, c = divmod(i, PASSES)
            nc.scalar.activation(
                out=dest[bt][:, c * K_PASS : (c + 1) * K_PASS].rearrange("p (b t) -> p b t", t=PACK),
                in_=z_t[i][:].rearrange("p t b -> p b t"), func=func, scale=scale,
            )

        def silu_of(i):
            z_function(i, silu, ACT.Silu, 1.0)

        def tanh_of(i):
            z_function(i, chain, ACT.Tanh, 0.5)

        def q_of(i):
            z_function(i, chain, ACT.Sigmoid, -1.0)

        w_codes = [keep.tile([P, DR], U32, name="w_codes%d" % c, align_bytes=64) for c in range(PASSES)]
        w_scales = [keep.tile([P, DR], U8, name="w_scales%d" % c, align_bytes=64) for c in range(PASSES)]
        w_grouped = {}

        def regroup_w(i, copy):
            width = w_pieces[i][2]
            w_grouped[i] = wg_pool.tile([P, width, PACK], BF16, name="w_grouped", align_bytes=64)
            copy(
                out=w_grouped[i][:].rearrange("p (q i) t -> p q t i", i=4),
                in_=w_raw[i][:].rearrange("p t (q i) -> p q t i", i=4),
            )

        def quantise_w(i):
            c, n0, width = w_pieces[i]
            nc.vector.quantize_mx(
                out=w_codes[c][:, n0 : n0 + width].bitcast(E4M3_X4),
                scales=w_scales[c][:, n0 : n0 + width],
                in_=w_grouped[i][:].rearrange("p n t -> p (n t)"),
            )

        def k_cols(c0, n):
            return slice(c0 * K_PASS, (c0 + n) * K_PASS)

        def square_of(bt, c0, n):
            view = chain[bt][:, k_cols(c0, n)]
            nc.scalar.activation(out=view, in_=view, func=ACT.Square, scale=-0.5, bias=half[:])

        def ln_of_q(bt, c0, n):
            view = chain[bt][:, k_cols(c0, n)]
            nc.scalar.activation(out=view, in_=view, func=ACT.Ln, bias=tiny[:])

        dz_codes = [keep.tile([P, PASSES * P], U32, name="dz_codes%d" % bt, align_bytes=64) for bt in range(B_TILES)]
        dz_scales = [keep.tile([P, PASSES * P], U8, name="dz_scales%d" % bt, align_bytes=64) for bt in range(B_TILES)]
        units = [(bt, c, 2) for bt in range(3) for c in (0, 2)] + [(3, c, 1) for c in range(4)]
        work = {}
        grad_t = {}
        dz_grouped = {}
        acc = {}

        def ratio(u):
            bt, c0, n = units[u]
            view = chain[bt][:, k_cols(c0, n)]
            nc.scalar.activation(out=view, in_=view, func=ACT.Sigmoid, scale=-1.0 if u < 5 and u not in CAPPED else -2.0)

        CAPPED = {3:5,4:6}

        def cap(bt, c0, n):
            view = chain[bt][:, k_cols(c0, n)]
            nc.vector.tensor_scalar_min(out=view, in0=view, scalar1=1.0 - 2.0**-24)

        def ln_unit(u):
            if u in CAPPED:
                bt, c0, n = units[u]
                view = chain[bt][:, k_cols(c0, n)]
                nc.scalar.activation(out=view, in_=view, func=ACT.Ln, scale=-0.5, bias=half[:])
            else:
                ln_of_q(*units[u])

        def turn_grad(u):
            bt, c0, n = units[u]
            grad_t[u] = psum_g.tile([P, PACK, n * P], BF16, name="grad_t")
            for c in range(n):
                for t in range(PACK):
                    k0 = (c0 + c) * K_PASS + t * P
                    nc.tensor.matmul(
                        grad_t[u][:, t, c * P : (c + 1) * P], lhsT=grad[bt][:, k0 : k0 + P], rhs=minus_four[:],
                        start=True, stop=True,
                    )

        def first_factor(u):
            bt, c0, n = units[u]
            work[u] = u_pool.tile([P, n * K_PASS], F32, name="work")
            nc.vector.scalar_tensor_tensor(
                out=work[u][:], in0=chain[bt][:, k_cols(c0, n)], scalar=1.0, in1=silu[bt][:, k_cols(c0, n)],
                op0=ALU.subtract, op1=ALU.mult,
            )

        def product(u):
            bt, c0, n = units[u]
            nc.vector.scalar_tensor_tensor(
                out=work[u][:], in0=work[u][:], scalar=0.5, in1=chain[bt][:, k_cols(c0, n)],
                op0=ALU.subtract, op1=ALU.mult,
            )

        def times_grad(u):
            dz_grouped[u] = dz_pool.tile([P, units[u][2] * P, PACK], BF16, name="dz_grouped", align_bytes=64)
            nc.vector.scalar_tensor_tensor(
                out=dz_grouped[u][:],
                in0=work[u][:].rearrange("p (x t) -> p x t", t=PACK),
                scalar=0.25,
                in1=grad_t[u][:].rearrange("p t x -> p x t"),
                op0=ALU.add,
                op1=ALU.mult,
            )

        def quantise_dz(u):
            bt, c0, n = units[u]
            cols = slice(c0 * P, (c0 + n) * P)
            nc.vector.quantize_mx(
                out=dz_codes[bt][:, cols].bitcast(E5M2_X4),
                scales=dz_scales[bt][:, cols],
                in_=dz_grouped[u][:].rearrange("p x t -> p (x t)"),
            )

        def multiply(bt, c, j):
            if c == 0:
                acc[bt, j] = psum.tile([P, N_TILE], F32, name="acc", tag="bank")
            nc.tensor.matmul_mx(
                out=acc[bt, j][:],
                lhsT=dz_codes[bt][:, c * P : (c + 1) * P].bitcast(E5M2_X4),
                lhsT_scale=dz_scales[bt][:, c * P : (c + 1) * P],
                rhs=w_codes[c][:, j * N_TILE : (j + 1) * N_TILE].bitcast(E4M3_X4),
                rhs_scale=w_scales[c][:, j * N_TILE : (j + 1) * N_TILE],
                start=(c == 0),
                stop=(c == PASSES - 1),
            )

        def multiply_unit(u, tiles):
            bt, c0, n = units[u]
            for j in tiles:
                for c in range(c0, c0 + n):
                    multiply(bt, c, j)

        def store(bt, j, copy):
            o_sb = o_pool.tile([P, N_TILE], F32, name="o_sb")
            copy(out=o_sb[:], in_=acc[bt, j][:])
            nc.sync.dma_start(out=out[rows(bt), j * N_TILE : (j + 1) * N_TILE], in_=o_sb[:])

        def store_rows(bt):
            for j in range(N_TILES):
                store(bt, j, nc.scalar.copy)

        ALL_TILES = range(N_TILES)
        HEAD = 10
        for i in range(B_TILES * PASSES):
            turn_z(i)
            silu_of(i)
            if i < HEAD:
                tanh_of(i)
            if i < HEAD and i % 2 == 1 and i // 2 not in CAPPED:
                square_of(i // PASSES, i % PASSES - 1, 2)
        LATE_W = len(w_pieces) - 1
        for i in range(LATE_W):
            regroup_w(i, nc.vector.tensor_copy)
            if i > 0:
                quantise_w(i - 1)
            if i in CAPPED.values():
                cap(*units[[u for u in CAPPED if CAPPED[u] == i][0]])
        for u in range(5):
            ln_unit(u)
        for u in range(5):
            ratio(u)
            if u in [1]:
                regroup_w(LATE_W + [1].index(u), nc.scalar.copy)
        turn_grad(0)
        turn_grad(1)
        for i in range(HEAD, B_TILES * PASSES):
            turn_z(i)
            q_of(i)
        for u in range(5, 6):
            ln_unit(u)
        ln_of_q(3, 0, PASSES)
        for u in range(5, 6):
            ratio(u)
        LAST = len(units) - 1
        for u in range(len(units)):
            first_factor(u)
            if u in [2]:
                quantise_w(LATE_W + [2].index(u))
            if u == 0:
                quantise_w(LATE_W - 1)
            else:
                times_grad(u - 1)
                if u + 1 <= LAST:
                    turn_grad(u + 1)
            product(u)
            if u > 0:
                quantise_dz(u - 1)
                if u == 3:
                    multiply_unit(2, [0, 1])
                elif u == 4:
                    multiply_unit(3, [0, 1])
                    multiply_unit(2, [2, 3])
                    multiply_unit(3, [2, 3])
                else:
                    multiply_unit(u - 1, ALL_TILES)
                if u == 4:
                    for v in range(6, len(units)):
                        ratio(v)
                if units[u][0] > units[u - 1][0]:
                    store_rows(units[u - 1][0])
        times_grad(LAST)
        quantise_dz(LAST)
        for j in ALL_TILES:
            multiply_unit(LAST, [j])
            store(B_TILES - 1, j, nc.vector.tensor_copy if j % 2 else nc.scalar.copy)
